import numpy as np
import ml_dtypes


def mxq(x, axis, fmt="e4m3"):
    dtype, down = {"e4m3": (ml_dtypes.float8_e4m3fn, 7), "e5m2": (ml_dtypes.float8_e5m2, 14)}[fmt]
    v = np.moveaxis(np.asarray(x, np.float32).astype(ml_dtypes.bfloat16).astype(np.float64), axis, -1)
    blocks = v.reshape(v.shape[:-1] + (-1, 32))
    amax = np.abs(blocks).max(-1, keepdims=True)
    byte = np.maximum(np.where(amax > 0, np.frexp(amax)[1] - 1 + 127, 0) - down, 1)
    scale = np.exp2(byte - 127.0)
    codes = (blocks / scale).astype(np.float32).astype(dtype).astype(np.float64)
    return np.moveaxis((codes * scale).reshape(v.shape), -1, axis)


WIDE = False


def mx_kscale(k):
    if not WIDE:
        return np.ones(k)
    levels = np.array([10, -10, 5, -5, 0])
    a = np.random.permutation(np.resize(levels, k // 512 * 4)).reshape(k // 512, 4)
    idx = np.arange(k)
    return np.exp2(a[idx // 512, idx % 128 // 32])


BF16 = ml_dtypes.bfloat16


def bf(x):
    return np.asarray(x, np.float32).astype(BF16)


def f64(x):
    return np.asarray(x).astype(np.float64)


E2M1 = np.array([0.0, 0.5, 1.0, 1.5, 2.0, 3.0, 4.0, 6.0, -0.0, -0.5, -1.0, -1.5, -2.0, -3.0, -4.0, -6.0])


def pack_weight(w, fmt):
    k, n = w.shape
    w = f64(bf(w)).reshape(k // 32, 32, n)
    amax = np.abs(w).max(1)
    if fmt == "e4m3":
        byte = np.frexp(amax)[1] - 1 + 127 - 7
    else:
        mant, ex = np.frexp(amax / 6.0)
        byte = np.where(mant > 0.5, ex, ex - 1) + 127
    byte = np.clip(np.where(amax > 0, byte, 1), 1, 254)
    scaled = (w * np.exp2(127.0 - byte)[:, None, :]).reshape(k, n).astype(np.float32)
    by_word = np.ascontiguousarray(scaled.reshape(k // 512, 128, 4, n).transpose(0, 1, 3, 2))
    if fmt == "e4m3":
        words = by_word.astype(ml_dtypes.float8_e4m3fn).view(np.uint8)
    else:
        c = by_word.astype(ml_dtypes.float4_e2m1fn).view(np.uint8) & 0xF
        words = c[..., 0::2] | (c[..., 1::2] << 4)
    return np.ascontiguousarray(words), np.ascontiguousarray(byte.astype(np.uint8).reshape(k // 512, 16, n))


def unpack_weight(words, scales, fmt):
    g, p, n, _ = words.shape
    if fmt == "e4m3":
        vals = np.ascontiguousarray(words).view(ml_dtypes.float8_e4m3fn).astype(np.float64)
    else:
        nib = np.empty((g, p, n, 4), np.uint8)
        nib[..., 0::2] = words & 0xF
        nib[..., 1::2] = words >> 4
        vals = E2M1[nib]
    vals = vals * np.repeat(np.exp2(scales.astype(np.float64) - 127.0), 8, axis=1)[..., None]
    return vals.transpose(0, 1, 3, 2).reshape(g * 512, n)


N, MI, MO, LMAX = 1024, 512, 128, 3
C = (LMAX + 1) ** 2
FMT = "e4m3"


def setup_inputs():
    s = mx_kscale(MI)
    d = {"x": bf(np.random.standard_normal((N, MI, C)) * s[None, :, None])}
    for l in range(LMAX + 1):
        words, scales = pack_weight(np.random.standard_normal((MI, MO)) / np.sqrt(MI) / s[:, None], FMT)
        d["w%d_words" % l] = words
        d["w%d_scales" % l] = scales
    return d


def reference(x, w0_words, w0_scales, w1_words, w1_scales, w2_words, w2_scales, w3_words, w3_scales):
    xq = mxq(f64(x), 1, "e4m3")
    parts = []
    packed = [(w0_words, w0_scales), (w1_words, w1_scales), (w2_words, w2_scales), (w3_words, w3_scales)]
    for l, (words, scales) in enumerate(packed):
        xl = xq[:, :, l * l:(l + 1) ** 2].transpose(0, 2, 1)
        parts.append((xl @ unpack_weight(words, scales, FMT)).transpose(0, 2, 1))
    return np.concatenate(parts, axis=2)

@@ -1,0 +1,113 @@
+from contextlib import ExitStack
+
+import concourse.mybir as mybir
+from concourse.masks import make_identity
+
+BF16 = mybir.dt.bfloat16
+F32 = mybir.dt.float32
+I32 = mybir.dt.int32
+U8 = mybir.dt.uint8
+U32 = mybir.dt.uint32
+FP8X4 = mybir.dt.float8_e4m3fn_x4
+
+P = 128
+PACK = 4
+ROWS = 1024
+K = 512
+OUTS = 128
+CHANNELS = 16
+DEGREES = 4
+DEGREE_OF_CHANNEL = [l for l in range(DEGREES) for m in range(2 * l + 1)]
+
+PAIRS = CHANNELS // 2
+QUAD = 4
+ROW_TILES = ROWS // P
+
+FLOPS = 2 * ROWS * K * OUTS * CHANNELS
+
+
+def tile_irrepsstridelinear_kernel(
+    tc, x, w0_words, w0_scales, w1_words, w1_scales, w2_words, w2_scales, w3_words, w3_scales, out
+):
+    nc = tc.nc
+    weights = [(w0_words, w0_scales), (w1_words, w1_scales), (w2_words, w2_scales), (w3_words, w3_scales)]
+
+    with ExitStack() as ctx:
+        keep = ctx.enter_context(tc.tile_pool(name="keep", bufs=1))
+        x_pool = ctx.enter_context(tc.tile_pool(name="x_pool", bufs=3))
+        mx_pool = ctx.enter_context(tc.tile_pool(name="mx_pool", bufs=2))
+        out_pool = ctx.enter_context(tc.tile_pool(name="out_pool", bufs=2))
+        xt_psum = ctx.enter_context(tc.psum_pool(name="xt_psum", bufs=6))
+        acc_psum = ctx.enter_context(tc.psum_pool(name="acc_psum", bufs=2))
+
+        identity = keep.tile([P, P], F32)
+        make_identity(nc, identity[:])
+
+        w_codes = keep.tile([P, DEGREES, PACK * OUTS], U8, align_bytes=64)
+        w_planes = keep.tile([P, DEGREES, OUTS], U8, align_bytes=64)
+        nc.vector.memset(w_planes[:].rearrange("p l o -> p (l o)").bitcast(I32), 0)
+
+        def load_rows(r):
+            x_sb = x_pool.tile([P, K * CHANNELS], BF16, name="x_sb")
+            nc.sync.dma_start(out=x_sb[:], in_=x[r * P : (r + 1) * P].rearrange("n i c -> n (i c)"))
+            return x_sb
+
+        first_rows = load_rows(0)
+
+        for l, (words, scales) in enumerate(weights):
+            nc.sync.dma_start(
+                out=w_codes[:, l, :].bitcast(I32),
+                in_=words.rearrange("g p o t -> (g p) (o t)").bitcast(I32),
+            )
+            for quadrant in range(4):
+                nc.sync.dma_start(
+                    out=w_planes[32 * quadrant : 32 * quadrant + 4, l, :].bitcast(I32),
+                    in_=scales.rearrange("g q o -> (g q) o")[4 * quadrant : 4 * quadrant + 4, :].bitcast(I32),
+                )
+
+        for r in range(ROW_TILES):
+            x_sb = first_rows if r == 0 else load_rows(r)
+            x_words = x_sb[:].bitcast(F32).rearrange("n (p t j) -> n t j p", t=PACK, j=PAIRS)
+
+            grouped = mx_pool.tile([P, CHANNELS, P, PACK], BF16, align_bytes=64)
+            codes = mx_pool.tile([P, CHANNELS, P], U32, align_bytes=64)
+            planes = mx_pool.tile([P, CHANNELS, P], U8, align_bytes=64)
+            out_sb = out_pool.tile([P, OUTS, CHANNELS], F32)
+
+            for q in range(CHANNELS // QUAD):
+                for j in range(2 * q, 2 * q + 2):
+                    xt = xt_psum.tile([P, PACK, P], F32)
+                    for t in range(PACK):
+                        nc.tensor.transpose(xt[:, t, :], x_words[:, t, j, :], identity[:])
+                    split = xt[:].bitcast(BF16).rearrange("p t (n e) -> p e n t", e=2)
+                    if j % 4 == 3:
+                        nc.vector.tensor_copy(out=grouped[:, 2 * j : 2 * j + 2, :, :], in_=split)
+                    else:
+                        nc.scalar.copy(out=grouped[:, 2 * j : 2 * j + 2, :, :], in_=split)
+
+                quad = slice(QUAD * q, QUAD * (q + 1))
+                nc.vector.quantize_mx(
+                    out=codes[:, quad, :].rearrange("p c n -> p (c n)").bitcast(FP8X4),
+                    scales=planes[:, quad, :].rearrange("p c n -> p (c n)"),
+                    in_=grouped[:, quad, :, :].rearrange("p c n t -> p (c n t)"),
+                )
+
+                acc = acc_psum.tile([P, QUAD, OUTS], F32)
+                for m in range(QUAD):
+                    c = QUAD * q + m
+                    l = DEGREE_OF_CHANNEL[c]
+                    nc.tensor.matmul_mx(
+                        out=acc[:, m, :],
+                        lhsT=codes[:, c, :].bitcast(FP8X4),
+                        lhsT_scale=planes[:, c, :],
+                        rhs=w_codes[:, l, :].bitcast(FP8X4),
+                        rhs_scale=w_planes[:, l, :],
+                        start=True,
+                        stop=True,
+                    )
+                nc.vector.tensor_copy(out=out_sb[:, :, quad], in_=acc[:].rearrange("p c o -> p o c"))
+
+            nc.sync.dma_start(
+                out=out[r * P : (r + 1) * P].rearrange("n o c -> n (o c)"),
+                in_=out_sb[:].rearrange("p o c -> p (o c)"),
+            )

@@ -22,6 +22,9 @@ DEGREE_OF_CHANNEL = [l for l in range(DEGREES) for m in range(2 * l + 1)]
 PAIRS = CHANNELS // 2
 QUAD = 4
 ROW_TILES = ROWS // P
+HALF = CHANNELS // 2
+STEPS = 2 * ROW_TILES
+LOADS_AHEAD = 3
 
 FLOPS = 2 * ROWS * K * OUTS * CHANNELS
 
@@ -34,11 +37,12 @@ def tile_irrepsstridelinear_kernel(
 
     with ExitStack() as ctx:
         keep = ctx.enter_context(tc.tile_pool(name="keep", bufs=1))
-        x_pool = ctx.enter_context(tc.tile_pool(name="x_pool", bufs=3))
+        x_pool = ctx.enter_context(tc.tile_pool(name="x_pool", bufs=LOADS_AHEAD + 1))
         mx_pool = ctx.enter_context(tc.tile_pool(name="mx_pool", bufs=2))
         out_pool = ctx.enter_context(tc.tile_pool(name="out_pool", bufs=2))
         xt_psum = ctx.enter_context(tc.psum_pool(name="xt_psum", bufs=6))
         acc_psum = ctx.enter_context(tc.psum_pool(name="acc_psum", bufs=2))
+        ctx.enter_context(tc.manual_schedule())
 
         identity = keep.tile([P, P], F32)
         make_identity(nc, identity[:])
@@ -47,55 +51,70 @@ def tile_irrepsstridelinear_kernel(
         w_planes = keep.tile([P, DEGREES, OUTS], U8, align_bytes=64)
         nc.vector.memset(w_planes[:].rearrange("p l o -> p (l o)").bitcast(I32), 0)
 
+        x_tiles = {}
+        out_tiles = {}
+        xt_banks = {}
+        grouped_tiles = {}
+        code_tiles = {}
+        acc_banks = {}
+
         def load_rows(r):
-            x_sb = x_pool.tile([P, K * CHANNELS], BF16, name="x_sb")
+            x_sb = x_pool.tile([P, K * CHANNELS], BF16)
             nc.sync.dma_start(out=x_sb[:], in_=x[r * P : (r + 1) * P].rearrange("n i c -> n (i c)"))
-            return x_sb
+            x_tiles[r] = x_sb
 
-        first_rows = load_rows(0)
-
-        for l, (words, scales) in enumerate(weights):
-            nc.sync.dma_start(
-                out=w_codes[:, l, :].bitcast(I32),
-                in_=words.rearrange("g p o t -> (g p) (o t)").bitcast(I32),
-            )
-            for quadrant in range(4):
+        def load_weights():
+            for l, (words, scales) in enumerate(weights):
                 nc.sync.dma_start(
-                    out=w_planes[32 * quadrant : 32 * quadrant + 4, l, :].bitcast(I32),
-                    in_=scales.rearrange("g q o -> (g q) o")[4 * quadrant : 4 * quadrant + 4, :].bitcast(I32),
+                    out=w_codes[:, l, :].bitcast(I32),
+                    in_=words.rearrange("g p o t -> (g p) (o t)").bitcast(I32),
                 )
+                for quadrant in range(4):
+                    nc.sync.dma_start(
+                        out=w_planes[32 * quadrant : 32 * quadrant + 4, l, :].bitcast(I32),
+                        in_=scales.rearrange("g q o -> (g q) o")[4 * quadrant : 4 * quadrant + 4, :].bitcast(I32),
+                    )
 
-        for r in range(ROW_TILES):
-            x_sb = first_rows if r == 0 else load_rows(r)
-            x_words = x_sb[:].bitcast(F32).rearrange("n (p t j) -> n t j p", t=PACK, j=PAIRS)
+        def transpose_half(s):
+            x_words = x_tiles[s // 2][:].bitcast(F32).rearrange("n (p t j) -> n t j p", t=PACK, j=PAIRS)
+            xt_banks[s] = []
+            for b in range(HALF // 2):
+                j = (s % 2) * (HALF // 2) + b
+                xt = xt_psum.tile([P, PACK, P], F32)
+                for t in range(PACK):
+                    nc.tensor.transpose(xt[:, t, :], x_words[:, t, j, :], identity[:])
+                xt_banks[s].append(xt)
 
-            grouped = mx_pool.tile([P, CHANNELS, P, PACK], BF16, align_bytes=64)
-            codes = mx_pool.tile([P, CHANNELS, P], U32, align_bytes=64)
-            planes = mx_pool.tile([P, CHANNELS, P], U8, align_bytes=64)
-            out_sb = out_pool.tile([P, OUTS, CHANNELS], F32)
+        def split_half(s):
+            grouped = mx_pool.tile([P, HALF, P, PACK], BF16, align_bytes=64)
+            grouped_tiles[s] = grouped
+            for b, xt in enumerate(xt_banks[s]):
+                split = xt[:].bitcast(BF16).rearrange("p t (n e) -> p e n t", e=2)
+                if b < 3:
+                    nc.scalar.copy(out=grouped[:, 2 * b : 2 * b + 2, :, :], in_=split)
+                else:
+                    nc.vector.tensor_copy(out=grouped[:, 2 * b : 2 * b + 2, :, :], in_=split)
 
-            for q in range(CHANNELS // QUAD):
-                for j in range(2 * q, 2 * q + 2):
-                    xt = xt_psum.tile([P, PACK, P], F32)
-                    for t in range(PACK):
-                        nc.tensor.transpose(xt[:, t, :], x_words[:, t, j, :], identity[:])
-                    split = xt[:].bitcast(BF16).rearrange("p t (n e) -> p e n t", e=2)
-                    if j % 4 == 3:
-                        nc.vector.tensor_copy(out=grouped[:, 2 * j : 2 * j + 2, :, :], in_=split)
-                    else:
-                        nc.scalar.copy(out=grouped[:, 2 * j : 2 * j + 2, :, :], in_=split)
-
+        def quantise_half(s):
+            codes = mx_pool.tile([P, HALF, P], U32, align_bytes=64)
+            planes = mx_pool.tile([P, HALF, P], U8, align_bytes=64)
+            code_tiles[s] = (codes, planes)
+            for q in range(HALF // QUAD):
                 quad = slice(QUAD * q, QUAD * (q + 1))
                 nc.vector.quantize_mx(
                     out=codes[:, quad, :].rearrange("p c n -> p (c n)").bitcast(FP8X4),
                     scales=planes[:, quad, :].rearrange("p c n -> p (c n)"),
-                    in_=grouped[:, quad, :, :].rearrange("p c n t -> p (c n t)"),
+                    in_=grouped_tiles[s][:, quad, :, :].rearrange("p c n t -> p (c n t)"),
                 )
 
+        def multiply_half(s):
+            codes, planes = code_tiles[s]
+            acc_banks[s] = []
+            for q in range(HALF // QUAD):
                 acc = acc_psum.tile([P, QUAD, OUTS], F32)
                 for m in range(QUAD):
                     c = QUAD * q + m
-                    l = DEGREE_OF_CHANNEL[c]
+                    l = DEGREE_OF_CHANNEL[(s % 2) * HALF + c]
                     nc.tensor.matmul_mx(
                         out=acc[:, m, :],
                         lhsT=codes[:, c, :].bitcast(FP8X4),
@@ -105,9 +124,39 @@ def tile_irrepsstridelinear_kernel(
                         start=True,
                         stop=True,
                     )
-                nc.vector.tensor_copy(out=out_sb[:, :, quad], in_=acc[:].rearrange("p c o -> p o c"))
+                acc_banks[s].append(acc)
 
-            nc.sync.dma_start(
-                out=out[r * P : (r + 1) * P].rearrange("n o c -> n (o c)"),
-                in_=out_sb[:].rearrange("p o c -> p (o c)"),
-            )
+        def store_half(s):
+            r = s // 2
+            if s % 2 == 0:
+                out_sb = out_pool.tile([P, OUTS, CHANNELS], F32)
+                out_tiles[r] = out_sb
+            for q, acc in enumerate(acc_banks[s]):
+                first = (s % 2) * HALF + QUAD * q
+                nc.vector.tensor_copy(
+                    out=out_tiles[r][:, :, first : first + QUAD], in_=acc[:].rearrange("p c o -> p o c")
+                )
+            if s % 2 == 1:
+                nc.sync.dma_start(
+                    out=out[r * P : (r + 1) * P].rearrange("n o c -> n (o c)"),
+                    in_=out_tiles[r][:].rearrange("p o c -> p (o c)"),
+                )
+
+        load_rows(0)
+        load_weights()
+        for r in range(1, LOADS_AHEAD):
+            load_rows(r)
+        transpose_half(0)
+
+        for s in range(STEPS + 1):
+            if s % 2 == 0 and s // 2 + LOADS_AHEAD < ROW_TILES:
+                load_rows(s // 2 + LOADS_AHEAD)
+            if s >= 1:
+                quantise_half(s - 1)
+                multiply_half(s - 1)
+            if s + 1 < STEPS:
+                transpose_half(s + 1)
+            if s < STEPS:
+                split_half(s)
+            if s >= 1:
+                store_half(s - 1)

@@ -38,14 +38,11 @@ def tile_irrepsstridelinear_kernel(
     with ExitStack() as ctx:
         keep = ctx.enter_context(tc.tile_pool(name="keep", bufs=1))
         x_pool = ctx.enter_context(tc.tile_pool(name="x_pool", bufs=LOADS_AHEAD + 1))
-        mx_pool = ctx.enter_context(tc.tile_pool(name="mx_pool", bufs=2))
-        out_pool = ctx.enter_context(tc.tile_pool(name="out_pool", bufs=2))
+        mx_pool = ctx.enter_context(tc.tile_pool(name="mx_pool", bufs=3))
+        out_pool = ctx.enter_context(tc.tile_pool(name="out_pool", bufs=3))
         xt_psum = ctx.enter_context(tc.psum_pool(name="xt_psum", bufs=6))
         acc_psum = ctx.enter_context(tc.psum_pool(name="acc_psum", bufs=2))
         ctx.enter_context(tc.manual_schedule())
-
-        identity = keep.tile([P, P], F32)
-        make_identity(nc, identity[:])
 
         w_codes = keep.tile([P, DEGREES, PACK * OUTS], U8, align_bytes=64)
         w_planes = keep.tile([P, DEGREES, OUTS], U8, align_bytes=64)
@@ -60,7 +57,7 @@ def tile_irrepsstridelinear_kernel(
 
         def load_rows(r):
             x_sb = x_pool.tile([P, K * CHANNELS], BF16)
-            nc.sync.dma_start(out=x_sb[:], in_=x[r * P : (r + 1) * P].rearrange("n i c -> n (i c)"))
+            nc.gpsimd.dma_start(out=x_sb[:], in_=x[r * P : (r + 1) * P].rearrange("n i c -> n (i c)"))
             x_tiles[r] = x_sb
 
         def load_weights():
@@ -90,7 +87,7 @@ def tile_irrepsstridelinear_kernel(
             grouped_tiles[s] = grouped
             for b, xt in enumerate(xt_banks[s]):
                 split = xt[:].bitcast(BF16).rearrange("p t (n e) -> p e n t", e=2)
-                if b < 3:
+                if b < 2:
                     nc.scalar.copy(out=grouped[:, 2 * b : 2 * b + 2, :, :], in_=split)
                 else:
                     nc.vector.tensor_copy(out=grouped[:, 2 * b : 2 * b + 2, :, :], in_=split)
@@ -133,9 +130,7 @@ def tile_irrepsstridelinear_kernel(
                 out_tiles[r] = out_sb
             for q, acc in enumerate(acc_banks[s]):
                 first = (s % 2) * HALF + QUAD * q
-                nc.vector.tensor_copy(
-                    out=out_tiles[r][:, :, first : first + QUAD], in_=acc[:].rearrange("p c o -> p o c")
-                )
+                nc.scalar.copy(out=out_tiles[r][:, :, first : first + QUAD], in_=acc[:].rearrange("p c o -> p o c"))
             if s % 2 == 1:
                 nc.sync.dma_start(
                     out=out[r * P : (r + 1) * P].rearrange("n o c -> n (o c)"),
@@ -143,20 +138,23 @@ def tile_irrepsstridelinear_kernel(
                 )
 
         load_rows(0)
+        identity = keep.tile([P, P], F32)
+        make_identity(nc, identity[:])
         load_weights()
         for r in range(1, LOADS_AHEAD):
             load_rows(r)
         transpose_half(0)
 
-        for s in range(STEPS + 1):
+        for s in range(STEPS + 2):
             if s % 2 == 0 and s // 2 + LOADS_AHEAD < ROW_TILES:
                 load_rows(s // 2 + LOADS_AHEAD)
-            if s >= 1:
+            if 1 <= s <= STEPS:
                 quantise_half(s - 1)
-                multiply_half(s - 1)
+            if s >= 2:
+                multiply_half(s - 2)
             if s + 1 < STEPS:
                 transpose_half(s + 1)
             if s < STEPS:
                 split_half(s)
-            if s >= 1:
-                store_half(s - 1)
+            if s >= 2:
+                store_half(s - 2)

@@ -24,7 +24,7 @@ QUAD = 4
 ROW_TILES = ROWS // P
 HALF = CHANNELS // 2
 STEPS = 2 * ROW_TILES
-LOADS_AHEAD = 3
+LOADS_AHEAD = DEGREES
 
 FLOPS = 2 * ROWS * K * OUTS * CHANNELS
 
@@ -57,20 +57,20 @@ def tile_irrepsstridelinear_kernel(
 
         def load_rows(r):
             x_sb = x_pool.tile([P, K * CHANNELS], BF16)
-            nc.gpsimd.dma_start(out=x_sb[:], in_=x[r * P : (r + 1) * P].rearrange("n i c -> n (i c)"))
+            nc.sync.dma_start(out=x_sb[:], in_=x[r * P : (r + 1) * P].rearrange("n i c -> n (i c)"))
             x_tiles[r] = x_sb
 
-        def load_weights():
-            for l, (words, scales) in enumerate(weights):
+        def load_weight(l):
+            words, scales = weights[l]
+            nc.sync.dma_start(
+                out=w_codes[:, l, :].bitcast(I32),
+                in_=words.rearrange("g p o t -> (g p) (o t)").bitcast(I32),
+            )
+            for quadrant in range(4):
                 nc.sync.dma_start(
-                    out=w_codes[:, l, :].bitcast(I32),
-                    in_=words.rearrange("g p o t -> (g p) (o t)").bitcast(I32),
+                    out=w_planes[32 * quadrant : 32 * quadrant + 4, l, :].bitcast(I32),
+                    in_=scales.rearrange("g q o -> (g q) o")[4 * quadrant : 4 * quadrant + 4, :].bitcast(I32),
                 )
-                for quadrant in range(4):
-                    nc.sync.dma_start(
-                        out=w_planes[32 * quadrant : 32 * quadrant + 4, l, :].bitcast(I32),
-                        in_=scales.rearrange("g q o -> (g q) o")[4 * quadrant : 4 * quadrant + 4, :].bitcast(I32),
-                    )
 
         def transpose_half(s):
             x_words = x_tiles[s // 2][:].bitcast(F32).rearrange("n (p t j) -> n t j p", t=PACK, j=PAIRS)
@@ -87,22 +87,20 @@ def tile_irrepsstridelinear_kernel(
             grouped_tiles[s] = grouped
             for b, xt in enumerate(xt_banks[s]):
                 split = xt[:].bitcast(BF16).rearrange("p t (n e) -> p e n t", e=2)
-                if b < 2:
-                    nc.scalar.copy(out=grouped[:, 2 * b : 2 * b + 2, :, :], in_=split)
-                else:
+                if b % 2 == 0:
                     nc.vector.tensor_copy(out=grouped[:, 2 * b : 2 * b + 2, :, :], in_=split)
+                else:
+                    nc.scalar.copy(out=grouped[:, 2 * b : 2 * b + 2, :, :], in_=split)
 
         def quantise_half(s):
             codes = mx_pool.tile([P, HALF, P], U32, align_bytes=64)
             planes = mx_pool.tile([P, HALF, P], U8, align_bytes=64)
             code_tiles[s] = (codes, planes)
-            for q in range(HALF // QUAD):
-                quad = slice(QUAD * q, QUAD * (q + 1))
-                nc.vector.quantize_mx(
-                    out=codes[:, quad, :].rearrange("p c n -> p (c n)").bitcast(FP8X4),
-                    scales=planes[:, quad, :].rearrange("p c n -> p (c n)"),
-                    in_=grouped_tiles[s][:, quad, :, :].rearrange("p c n t -> p (c n t)"),
-                )
+            nc.vector.quantize_mx(
+                out=codes[:].rearrange("p c n -> p (c n)").bitcast(FP8X4),
+                scales=planes[:].rearrange("p c n -> p (c n)"),
+                in_=grouped_tiles[s][:].rearrange("p c n t -> p (c n t)"),
+            )
 
         def multiply_half(s):
             codes, planes = code_tiles[s]
@@ -137,24 +135,23 @@ def tile_irrepsstridelinear_kernel(
                     in_=out_tiles[r][:].rearrange("p o c -> p (o c)"),
                 )
 
-        load_rows(0)
         identity = keep.tile([P, P], F32)
         make_identity(nc, identity[:])
-        load_weights()
-        for r in range(1, LOADS_AHEAD):
-            load_rows(r)
+        for l in range(DEGREES):
+            load_rows(l)
+            load_weight(l)
         transpose_half(0)
 
         for s in range(STEPS + 2):
             if s % 2 == 0 and s // 2 + LOADS_AHEAD < ROW_TILES:
                 load_rows(s // 2 + LOADS_AHEAD)
-            if 1 <= s <= STEPS:
-                quantise_half(s - 1)
             if s >= 2:
                 multiply_half(s - 2)
             if s + 1 < STEPS:
                 transpose_half(s + 1)
             if s < STEPS:
                 split_half(s)
+            if 1 <= s <= STEPS:
+                quantise_half(s - 1)
             if s >= 2:
                 store_half(s - 2)

@@ -24,7 +24,7 @@ QUAD = 4
 ROW_TILES = ROWS // P
 HALF = CHANNELS // 2
 STEPS = 2 * ROW_TILES
-LOADS_AHEAD = DEGREES
+LOADS_AHEAD = ROW_TILES
 
 FLOPS = 2 * ROWS * K * OUTS * CHANNELS
 
@@ -37,9 +37,9 @@ def tile_irrepsstridelinear_kernel(
 
     with ExitStack() as ctx:
         keep = ctx.enter_context(tc.tile_pool(name="keep", bufs=1))
-        x_pool = ctx.enter_context(tc.tile_pool(name="x_pool", bufs=LOADS_AHEAD + 1))
+        x_pool = ctx.enter_context(tc.tile_pool(name="x_pool", bufs=ROW_TILES))
         mx_pool = ctx.enter_context(tc.tile_pool(name="mx_pool", bufs=3))
-        out_pool = ctx.enter_context(tc.tile_pool(name="out_pool", bufs=3))
+        out_pool = ctx.enter_context(tc.tile_pool(name="out_pool", bufs=5))
         xt_psum = ctx.enter_context(tc.psum_pool(name="xt_psum", bufs=6))
         acc_psum = ctx.enter_context(tc.psum_pool(name="acc_psum", bufs=2))
         ctx.enter_context(tc.manual_schedule())
@@ -140,6 +140,8 @@ def tile_irrepsstridelinear_kernel(
         for l in range(DEGREES):
             load_rows(l)
             load_weight(l)
+        for r in range(DEGREES, ROW_TILES):
+            load_rows(r)
         transpose_half(0)
 
         for s in range(STEPS + 2):

@@ -42,7 +42,6 @@ def tile_irrepsstridelinear_kernel(
         out_pool = ctx.enter_context(tc.tile_pool(name="out_pool", bufs=5))
         xt_psum = ctx.enter_context(tc.psum_pool(name="xt_psum", bufs=6))
         acc_psum = ctx.enter_context(tc.psum_pool(name="acc_psum", bufs=2))
-        ctx.enter_context(tc.manual_schedule())
 
         w_codes = keep.tile([P, DEGREES, PACK * OUTS], U8, align_bytes=64)
         w_planes = keep.tile([P, DEGREES, OUTS], U8, align_bytes=64)

@@ -24,7 +24,8 @@ QUAD = 4
 ROW_TILES = ROWS // P
 HALF = CHANNELS // 2
 STEPS = 2 * ROW_TILES
-LOADS_AHEAD = ROW_TILES
+QUAD_CHANNELS = range(4, 8)
+FIRST_PAIRED = 3
 
 FLOPS = 2 * ROWS * K * OUTS * CHANNELS
 
@@ -38,8 +39,10 @@ def tile_irrepsstridelinear_kernel(
     with ExitStack() as ctx:
         keep = ctx.enter_context(tc.tile_pool(name="keep", bufs=1))
         x_pool = ctx.enter_context(tc.tile_pool(name="x_pool", bufs=ROW_TILES))
+        grouped_pool = ctx.enter_context(tc.tile_pool(name="grouped_pool", bufs=3))
+        pair_pool = ctx.enter_context(tc.tile_pool(name="pair_pool", bufs=2))
         mx_pool = ctx.enter_context(tc.tile_pool(name="mx_pool", bufs=3))
-        out_pool = ctx.enter_context(tc.tile_pool(name="out_pool", bufs=5))
+        out_pool = ctx.enter_context(tc.tile_pool(name="out_pool", bufs=4))
         xt_psum = ctx.enter_context(tc.psum_pool(name="xt_psum", bufs=6))
         acc_psum = ctx.enter_context(tc.psum_pool(name="acc_psum", bufs=2))
 
@@ -49,6 +52,7 @@ def tile_irrepsstridelinear_kernel(
 
         x_tiles = {}
         out_tiles = {}
+        pair_tiles = {}
         xt_banks = {}
         grouped_tiles = {}
         code_tiles = {}
@@ -71,25 +75,63 @@ def tile_irrepsstridelinear_kernel(
                     in_=scales.rearrange("g q o -> (g q) o")[4 * quadrant : 4 * quadrant + 4, :].bitcast(I32),
                 )
 
+        def paired(s):
+            return s % 2 == 0 and s // 2 >= FIRST_PAIRED
+
+        def pair_words(s):
+            r, half = (s + 3) // 2, (s + 3) % 2
+            if not (FIRST_PAIRED <= r < ROW_TILES):
+                return
+            if half == 0:
+                pairs = pair_pool.tile([P, QUAD, K], BF16)
+                pair_tiles[r] = pairs
+            first = QUAD_CHANNELS[0]
+            blocks = slice(half * (P // 2), (half + 1) * (P // 2))
+            nc.gpsimd.tensor_scalar(
+                out=pair_tiles[r][:].rearrange("n c (b i) -> n b c i", i=4)[:, blocks, :, :],
+                in0=x_tiles[r][:].rearrange("n (b i c) -> n b c i", i=4, c=CHANNELS)[
+                    :, blocks, first : first + QUAD, :
+                ],
+                scalar1=1.0,
+                scalar2=0.0,
+                op0=mybir.AluOpType.mult,
+                op1=mybir.AluOpType.add,
+            )
+
         def transpose_half(s):
             x_words = x_tiles[s // 2][:].bitcast(F32).rearrange("n (p t j) -> n t j p", t=PACK, j=PAIRS)
             xt_banks[s] = []
             for b in range(HALF // 2):
                 j = (s % 2) * (HALF // 2) + b
                 xt = xt_psum.tile([P, PACK, P], F32)
-                for t in range(PACK):
-                    nc.tensor.transpose(xt[:, t, :], x_words[:, t, j, :], identity[:])
+                if paired(s) and b >= 2:
+                    for m in range(2):
+                        for u in range(2):
+                            nc.tensor.transpose(
+                                xt[:, 2 * m + u, :], pair_tiles[s // 2][:, 2 * (b - 2) + m, :].bitcast(F32)[:, u::2], identity[:]
+                            )
+                else:
+                    for t in range(PACK):
+                        nc.tensor.transpose(xt[:, t, :], x_words[:, t, j, :], identity[:])
                 xt_banks[s].append(xt)
 
         def split_half(s):
-            grouped = mx_pool.tile([P, HALF, P, PACK], BF16, align_bytes=64)
+            grouped = grouped_pool.tile([P, HALF, P, PACK], BF16, align_bytes=64)
             grouped_tiles[s] = grouped
             for b, xt in enumerate(xt_banks[s]):
-                split = xt[:].bitcast(BF16).rearrange("p t (n e) -> p e n t", e=2)
-                if b % 2 == 0:
-                    nc.vector.tensor_copy(out=grouped[:, 2 * b : 2 * b + 2, :, :], in_=split)
+                two_channels = grouped[:, 2 * b : 2 * b + 2, :, :]
+                if paired(s) and b >= 2:
+                    source = xt[:].rearrange("p (m u) n -> p m n u", u=2)
+                    target = two_channels.rearrange("p m n t -> p (m n t)").bitcast(F32).rearrange(
+                        "p (m n u) -> p m n u", m=2, u=2
+                    )
                 else:
-                    nc.scalar.copy(out=grouped[:, 2 * b : 2 * b + 2, :, :], in_=split)
+                    source = xt[:].bitcast(BF16).rearrange("p t (n e) -> p e n t", e=2)
+                    target = two_channels
+                if b % 2 == 0:
+                    nc.vector.tensor_copy(out=target, in_=source)
+                else:
+                    nc.scalar.copy(out=target, in_=source)
 
         def quantise_half(s):
             codes = mx_pool.tile([P, HALF, P], U32, align_bytes=64)
@@ -141,11 +183,12 @@ def tile_irrepsstridelinear_kernel(
             load_weight(l)
         for r in range(DEGREES, ROW_TILES):
             load_rows(r)
+        ctx.enter_context(tc.manual_schedule())
         transpose_half(0)
 
         for s in range(STEPS + 2):
-            if s % 2 == 0 and s // 2 + LOADS_AHEAD < ROW_TILES:
-                load_rows(s // 2 + LOADS_AHEAD)
+            if s < STEPS:
+                pair_words(s)
             if s >= 2:
                 multiply_half(s - 2)
             if s + 1 < STEPS:

@@ -25,7 +25,7 @@ ROW_TILES = ROWS // P
 HALF = CHANNELS // 2
 STEPS = 2 * ROW_TILES
 QUAD_CHANNELS = range(4, 8)
-FIRST_PAIRED = 3
+FIRST_PAIRED = 2
 
 FLOPS = 2 * ROWS * K * OUTS * CHANNELS
 
@@ -40,13 +40,14 @@ def tile_irrepsstridelinear_kernel(
         keep = ctx.enter_context(tc.tile_pool(name="keep", bufs=1))
         x_pool = ctx.enter_context(tc.tile_pool(name="x_pool", bufs=ROW_TILES))
         grouped_pool = ctx.enter_context(tc.tile_pool(name="grouped_pool", bufs=3))
-        pair_pool = ctx.enter_context(tc.tile_pool(name="pair_pool", bufs=2))
+        pair_pool = ctx.enter_context(tc.tile_pool(name="pair_pool", bufs=4))
         mx_pool = ctx.enter_context(tc.tile_pool(name="mx_pool", bufs=3))
         out_pool = ctx.enter_context(tc.tile_pool(name="out_pool", bufs=4))
         xt_psum = ctx.enter_context(tc.psum_pool(name="xt_psum", bufs=6))
         acc_psum = ctx.enter_context(tc.psum_pool(name="acc_psum", bufs=2))
 
         w_codes = keep.tile([P, DEGREES, PACK * OUTS], U8, align_bytes=64)
+        w_swapped = keep.tile([P, PACK * OUTS], U8, align_bytes=64)
         w_planes = keep.tile([P, DEGREES, OUTS], U8, align_bytes=64)
         nc.vector.memset(w_planes[:].rearrange("p l o -> p (l o)").bitcast(I32), 0)
 
@@ -79,18 +80,16 @@ def tile_irrepsstridelinear_kernel(
             return s % 2 == 0 and s // 2 >= FIRST_PAIRED
 
         def pair_words(s):
-            r, half = (s + 3) // 2, (s + 3) % 2
+            r, u = (s + 3) // 2, (s + 3) % 2
             if not (FIRST_PAIRED <= r < ROW_TILES):
                 return
-            if half == 0:
-                pairs = pair_pool.tile([P, QUAD, K], BF16)
-                pair_tiles[r] = pairs
+            pairs = pair_pool.tile([P, QUAD, 2 * P], BF16)
+            pair_tiles[(r, u)] = pairs
             first = QUAD_CHANNELS[0]
-            blocks = slice(half * (P // 2), (half + 1) * (P // 2))
             nc.gpsimd.tensor_scalar(
-                out=pair_tiles[r][:].rearrange("n c (b i) -> n b c i", i=4)[:, blocks, :, :],
-                in0=x_tiles[r][:].rearrange("n (b i c) -> n b c i", i=4, c=CHANNELS)[
-                    :, blocks, first : first + QUAD, :
+                out=pairs[:].rearrange("n c (b i) -> n b c i", i=4),
+                in0=x_tiles[r][:].rearrange("n (b i v c) -> n v b c i", i=4, v=2, c=CHANNELS)[
+                    :, u, :, first : first + QUAD, :
                 ],
                 scalar1=1.0,
                 scalar2=0.0,
@@ -108,7 +107,7 @@ def tile_irrepsstridelinear_kernel(
                     for m in range(2):
                         for u in range(2):
                             nc.tensor.transpose(
-                                xt[:, 2 * m + u, :], pair_tiles[s // 2][:, 2 * (b - 2) + m, :].bitcast(F32)[:, u::2], identity[:]
+                                xt[:, 2 * m + u, :], pair_tiles[(s // 2, u)][:, 2 * (b - 2) + m, :].bitcast(F32), identity[:]
                             )
                 else:
                     for t in range(PACK):
@@ -133,29 +132,35 @@ def tile_irrepsstridelinear_kernel(
                 else:
                     nc.scalar.copy(out=target, in_=source)
 
-        def quantise_half(s):
+        def quantise_half(s, calls=1):
             codes = mx_pool.tile([P, HALF, P], U32, align_bytes=64)
             planes = mx_pool.tile([P, HALF, P], U8, align_bytes=64)
             code_tiles[s] = (codes, planes)
-            nc.vector.quantize_mx(
-                out=codes[:].rearrange("p c n -> p (c n)").bitcast(FP8X4),
-                scales=planes[:].rearrange("p c n -> p (c n)"),
-                in_=grouped_tiles[s][:].rearrange("p c n t -> p (c n t)"),
-            )
+            for part in range(calls):
+                channels = slice(part * HALF // calls, (part + 1) * HALF // calls)
+                nc.vector.quantize_mx(
+                    out=codes[:, channels, :].rearrange("p c n -> p (c n)").bitcast(FP8X4),
+                    scales=planes[:, channels, :].rearrange("p c n -> p (c n)"),
+                    in_=grouped_tiles[s][:, channels, :, :].rearrange("p c n t -> p (c n t)"),
+                )
 
         def multiply_half(s):
             codes, planes = code_tiles[s]
             acc_banks[s] = []
             for q in range(HALF // QUAD):
-                acc = acc_psum.tile([P, QUAD, OUTS], F32)
+                if s >= STEPS - 2:
+                    acc = xt_psum.tile([P, QUAD, OUTS], F32, name="xt")
+                else:
+                    acc = acc_psum.tile([P, QUAD, OUTS], F32)
                 for m in range(QUAD):
                     c = QUAD * q + m
                     l = DEGREE_OF_CHANNEL[(s % 2) * HALF + c]
+                    words = w_swapped[:] if paired(s) and q == 1 else w_codes[:, l, :]
                     nc.tensor.matmul_mx(
                         out=acc[:, m, :],
                         lhsT=codes[:, c, :].bitcast(FP8X4),
                         lhsT_scale=planes[:, c, :],
-                        rhs=w_codes[:, l, :].bitcast(FP8X4),
+                        rhs=words.bitcast(FP8X4),
                         rhs_scale=w_planes[:, l, :],
                         start=True,
                         stop=True,
@@ -176,26 +181,53 @@ def tile_irrepsstridelinear_kernel(
                     in_=out_tiles[r][:].rearrange("p o c -> p (o c)"),
                 )
 
+        def store_last():
+            s, r = STEPS - 1, ROW_TILES - 1
+            first = HALF
+            nc.scalar.copy(
+                out=out_tiles[r][:, :, first : first + QUAD], in_=acc_banks[s][0][:].rearrange("p c o -> p o c")
+            )
+            first += QUAD
+            for h in range(2):
+                o = slice(h * OUTS // 2, (h + 1) * OUTS // 2)
+                nc.vector.tensor_copy(
+                    out=out_tiles[r][:, o, first : first + QUAD],
+                    in_=acc_banks[s][1][:, :, o].rearrange("p c o -> p o c"),
+                )
+                nc.sync.dma_start(
+                    out=out[r * P : (r + 1) * P, o, :].rearrange("n o c -> n (o c)"),
+                    in_=out_tiles[r][:, o, :].rearrange("p o c -> p (o c)"),
+                )
+
         identity = keep.tile([P, P], F32)
         make_identity(nc, identity[:])
-        for l in range(DEGREES):
-            load_rows(l)
+        load_rows(0)
+        load_weight(2)
+        load_rows(1)
+        for l in (0, 1, 3):
             load_weight(l)
-        for r in range(DEGREES, ROW_TILES):
+        for r in range(2, ROW_TILES):
             load_rows(r)
+        nc.gpsimd.tensor_copy(
+            out=w_swapped[:].rearrange("p (o u e) -> p o e u", u=2, e=2),
+            in_=w_codes[:, 2, :].rearrange("p (o e u) -> p o e u", e=2, u=2),
+        )
         ctx.enter_context(tc.manual_schedule())
         transpose_half(0)
 
-        for s in range(STEPS + 2):
-            if s < STEPS:
-                pair_words(s)
+        for s in range(STEPS):
+            pair_words(s)
             if s >= 2:
                 multiply_half(s - 2)
             if s + 1 < STEPS:
                 transpose_half(s + 1)
-            if s < STEPS:
-                split_half(s)
-            if 1 <= s <= STEPS:
+            split_half(s)
+            if s >= 1:
                 quantise_half(s - 1)
             if s >= 2:
                 store_half(s - 2)
+        multiply_half(STEPS - 2)
+        quantise_half(STEPS - 1, calls=2)
+        store_half(STEPS - 2)
+        multiply_half(STEPS - 1)
+        store_last()

@@ -25,7 +25,7 @@ ROW_TILES = ROWS // P
 HALF = CHANNELS // 2
 STEPS = 2 * ROW_TILES
 QUAD_CHANNELS = range(4, 8)
-FIRST_PAIRED = 2
+FIRST_PAIRED = 3
 
 FLOPS = 2 * ROWS * K * OUTS * CHANNELS
 
@@ -203,10 +203,12 @@ def tile_irrepsstridelinear_kernel(
         make_identity(nc, identity[:])
         load_rows(0)
         load_weight(2)
+        load_weight(0)
         load_rows(1)
-        for l in (0, 1, 3):
-            load_weight(l)
-        for r in range(2, ROW_TILES):
+        load_weight(1)
+        load_rows(2)
+        load_weight(3)
+        for r in range(3, ROW_TILES):
             load_rows(r)
         nc.gpsimd.tensor_copy(
             out=w_swapped[:].rearrange("p (o u e) -> p o e u", u=2, e=2),

@@ -42,7 +42,7 @@ def tile_irrepsstridelinear_kernel(
         grouped_pool = ctx.enter_context(tc.tile_pool(name="grouped_pool", bufs=3))
         pair_pool = ctx.enter_context(tc.tile_pool(name="pair_pool", bufs=4))
         mx_pool = ctx.enter_context(tc.tile_pool(name="mx_pool", bufs=3))
-        out_pool = ctx.enter_context(tc.tile_pool(name="out_pool", bufs=4))
+        out_pool = ctx.enter_context(tc.tile_pool(name="out_pool", bufs=6))
         xt_psum = ctx.enter_context(tc.psum_pool(name="xt_psum", bufs=6))
         acc_psum = ctx.enter_context(tc.psum_pool(name="acc_psum", bufs=2))
 

@@ -24,8 +24,6 @@ QUAD = 4
 ROW_TILES = ROWS // P
 HALF = CHANNELS // 2
 STEPS = 2 * ROW_TILES
-QUAD_CHANNELS = range(4, 8)
-FIRST_PAIRED = 3
 
 FLOPS = 2 * ROWS * K * OUTS * CHANNELS
 
@@ -39,25 +37,24 @@ def tile_irrepsstridelinear_kernel(
     with ExitStack() as ctx:
         keep = ctx.enter_context(tc.tile_pool(name="keep", bufs=1))
         x_pool = ctx.enter_context(tc.tile_pool(name="x_pool", bufs=ROW_TILES))
-        grouped_pool = ctx.enter_context(tc.tile_pool(name="grouped_pool", bufs=3))
-        pair_pool = ctx.enter_context(tc.tile_pool(name="pair_pool", bufs=4))
         mx_pool = ctx.enter_context(tc.tile_pool(name="mx_pool", bufs=3))
         out_pool = ctx.enter_context(tc.tile_pool(name="out_pool", bufs=6))
         xt_psum = ctx.enter_context(tc.psum_pool(name="xt_psum", bufs=6))
         acc_psum = ctx.enter_context(tc.psum_pool(name="acc_psum", bufs=2))
 
         w_codes = keep.tile([P, DEGREES, PACK * OUTS], U8, align_bytes=64)
-        w_swapped = keep.tile([P, PACK * OUTS], U8, align_bytes=64)
         w_planes = keep.tile([P, DEGREES, OUTS], U8, align_bytes=64)
         nc.vector.memset(w_planes[:].rearrange("p l o -> p (l o)").bitcast(I32), 0)
 
         x_tiles = {}
         out_tiles = {}
-        pair_tiles = {}
         xt_banks = {}
         grouped_tiles = {}
         code_tiles = {}
         acc_banks = {}
+
+        def first_channel(s):
+            return HALF if s % 2 == 0 else 0
 
         def load_rows(r):
             x_sb = x_pool.tile([P, K * CHANNELS], BF16)
@@ -76,61 +73,25 @@ def tile_irrepsstridelinear_kernel(
                     in_=scales.rearrange("g q o -> (g q) o")[4 * quadrant : 4 * quadrant + 4, :].bitcast(I32),
                 )
 
-        def paired(s):
-            return s % 2 == 0 and s // 2 >= FIRST_PAIRED
-
-        def pair_words(s):
-            r, u = (s + 3) // 2, (s + 3) % 2
-            if not (FIRST_PAIRED <= r < ROW_TILES):
-                return
-            pairs = pair_pool.tile([P, QUAD, 2 * P], BF16)
-            pair_tiles[(r, u)] = pairs
-            first = QUAD_CHANNELS[0]
-            nc.gpsimd.tensor_scalar(
-                out=pairs[:].rearrange("n c (b i) -> n b c i", i=4),
-                in0=x_tiles[r][:].rearrange("n (b i v c) -> n v b c i", i=4, v=2, c=CHANNELS)[
-                    :, u, :, first : first + QUAD, :
-                ],
-                scalar1=1.0,
-                scalar2=0.0,
-                op0=mybir.AluOpType.mult,
-                op1=mybir.AluOpType.add,
-            )
-
         def transpose_half(s):
             x_words = x_tiles[s // 2][:].bitcast(F32).rearrange("n (p t j) -> n t j p", t=PACK, j=PAIRS)
             xt_banks[s] = []
             for b in range(HALF // 2):
-                j = (s % 2) * (HALF // 2) + b
+                j = first_channel(s) // 2 + b
                 xt = xt_psum.tile([P, PACK, P], F32)
-                if paired(s) and b >= 2:
-                    for m in range(2):
-                        for u in range(2):
-                            nc.tensor.transpose(
-                                xt[:, 2 * m + u, :], pair_tiles[(s // 2, u)][:, 2 * (b - 2) + m, :].bitcast(F32), identity[:]
-                            )
-                else:
-                    for t in range(PACK):
-                        nc.tensor.transpose(xt[:, t, :], x_words[:, t, j, :], identity[:])
+                for t in range(PACK):
+                    nc.tensor.transpose(xt[:, t, :], x_words[:, t, j, :], identity[:])
                 xt_banks[s].append(xt)
 
         def split_half(s):
-            grouped = grouped_pool.tile([P, HALF, P, PACK], BF16, align_bytes=64)
+            grouped = mx_pool.tile([P, HALF, P, PACK], BF16, align_bytes=64)
             grouped_tiles[s] = grouped
             for b, xt in enumerate(xt_banks[s]):
-                two_channels = grouped[:, 2 * b : 2 * b + 2, :, :]
-                if paired(s) and b >= 2:
-                    source = xt[:].rearrange("p (m u) n -> p m n u", u=2)
-                    target = two_channels.rearrange("p m n t -> p (m n t)").bitcast(F32).rearrange(
-                        "p (m n u) -> p m n u", m=2, u=2
-                    )
-                else:
-                    source = xt[:].bitcast(BF16).rearrange("p t (n e) -> p e n t", e=2)
-                    target = two_channels
+                split = xt[:].bitcast(BF16).rearrange("p t (n e) -> p e n t", e=2)
                 if b % 2 == 0:
-                    nc.vector.tensor_copy(out=target, in_=source)
+                    nc.vector.tensor_copy(out=grouped[:, 2 * b : 2 * b + 2, :, :], in_=split)
                 else:
-                    nc.scalar.copy(out=target, in_=source)
+                    nc.scalar.copy(out=grouped[:, 2 * b : 2 * b + 2, :, :], in_=split)
 
         def quantise_half(s, calls=1):
             codes = mx_pool.tile([P, HALF, P], U32, align_bytes=64)
@@ -154,13 +115,12 @@ def tile_irrepsstridelinear_kernel(
                     acc = acc_psum.tile([P, QUAD, OUTS], F32)
                 for m in range(QUAD):
                     c = QUAD * q + m
-                    l = DEGREE_OF_CHANNEL[(s % 2) * HALF + c]
-                    words = w_swapped[:] if paired(s) and q == 1 else w_codes[:, l, :]
+                    l = DEGREE_OF_CHANNEL[first_channel(s) + c]
                     nc.tensor.matmul_mx(
                         out=acc[:, m, :],
                         lhsT=codes[:, c, :].bitcast(FP8X4),
                         lhsT_scale=planes[:, c, :],
-                        rhs=words.bitcast(FP8X4),
+                        rhs=w_codes[:, l, :].bitcast(FP8X4),
                         rhs_scale=w_planes[:, l, :],
                         start=True,
                         stop=True,
@@ -173,7 +133,7 @@ def tile_irrepsstridelinear_kernel(
                 out_sb = out_pool.tile([P, OUTS, CHANNELS], F32)
                 out_tiles[r] = out_sb
             for q, acc in enumerate(acc_banks[s]):
-                first = (s % 2) * HALF + QUAD * q
+                first = first_channel(s) + QUAD * q
                 nc.scalar.copy(out=out_tiles[r][:, :, first : first + QUAD], in_=acc[:].rearrange("p c o -> p o c"))
             if s % 2 == 1:
                 nc.sync.dma_start(
@@ -183,7 +143,7 @@ def tile_irrepsstridelinear_kernel(
 
         def store_last():
             s, r = STEPS - 1, ROW_TILES - 1
-            first = HALF
+            first = first_channel(s)
             nc.scalar.copy(
                 out=out_tiles[r][:, :, first : first + QUAD], in_=acc_banks[s][0][:].rearrange("p c o -> p o c")
             )
@@ -203,22 +163,17 @@ def tile_irrepsstridelinear_kernel(
         make_identity(nc, identity[:])
         load_rows(0)
         load_weight(2)
-        load_weight(0)
         load_rows(1)
-        load_weight(1)
-        load_rows(2)
         load_weight(3)
+        load_rows(2)
+        load_weight(0)
+        load_weight(1)
         for r in range(3, ROW_TILES):
             load_rows(r)
-        nc.gpsimd.tensor_copy(
-            out=w_swapped[:].rearrange("p (o u e) -> p o e u", u=2, e=2),
-            in_=w_codes[:, 2, :].rearrange("p (o e u) -> p o e u", e=2, u=2),
-        )
         ctx.enter_context(tc.manual_schedule())
         transpose_half(0)
 
         for s in range(STEPS):
-            pair_words(s)
             if s >= 2:
                 multiply_half(s - 2)
             if s + 1 < STEPS:

from contextlib import ExitStack

import concourse.mybir as mybir
from concourse.masks import make_identity

BF16 = mybir.dt.bfloat16
F32 = mybir.dt.float32
I32 = mybir.dt.int32
U8 = mybir.dt.uint8
U32 = mybir.dt.uint32
FP8X4 = mybir.dt.float8_e4m3fn_x4

P = 128
PACK = 4
ROWS = 1024
K = 512
OUTS = 128
CHANNELS = 16
DEGREES = 4
DEGREE_OF_CHANNEL = [l for l in range(DEGREES) for m in range(2 * l + 1)]

PAIRS = CHANNELS // 2
QUAD = 4
ROW_TILES = ROWS // P
HALF = CHANNELS // 2
STEPS = 2 * ROW_TILES

FLOPS = 2 * ROWS * K * OUTS * CHANNELS


def tile_irrepsstridelinear_kernel(
    tc, x, w0_words, w0_scales, w1_words, w1_scales, w2_words, w2_scales, w3_words, w3_scales, out
):
    nc = tc.nc
    weights = [(w0_words, w0_scales), (w1_words, w1_scales), (w2_words, w2_scales), (w3_words, w3_scales)]

    with ExitStack() as ctx:
        keep = ctx.enter_context(tc.tile_pool(name="keep", bufs=1))
        x_pool = ctx.enter_context(tc.tile_pool(name="x_pool", bufs=ROW_TILES))
        mx_pool = ctx.enter_context(tc.tile_pool(name="mx_pool", bufs=3))
        out_pool = ctx.enter_context(tc.tile_pool(name="out_pool", bufs=6))
        xt_psum = ctx.enter_context(tc.psum_pool(name="xt_psum", bufs=6))
        acc_psum = ctx.enter_context(tc.psum_pool(name="acc_psum", bufs=2))

        w_codes = keep.tile([P, DEGREES, PACK * OUTS], U8, align_bytes=64)
        w_planes = keep.tile([P, DEGREES, OUTS], U8, align_bytes=64)
        nc.vector.memset(w_planes[:].rearrange("p l o -> p (l o)").bitcast(I32), 0)

        x_tiles = {}
        out_tiles = {}
        xt_banks = {}
        grouped_tiles = {}
        code_tiles = {}
        acc_banks = {}

        def first_channel(s):
            return HALF if s % 2 == 0 else 0

        def load_rows(r):
            x_sb = x_pool.tile([P, K * CHANNELS], BF16)
            nc.sync.dma_start(out=x_sb[:], in_=x[r * P : (r + 1) * P].rearrange("n i c -> n (i c)"))
            x_tiles[r] = x_sb

        def load_weight(l):
            words, scales = weights[l]
            nc.sync.dma_start(
                out=w_codes[:, l, :].bitcast(I32),
                in_=words.rearrange("g p o t -> (g p) (o t)").bitcast(I32),
            )
            for quadrant in range(4):
                nc.sync.dma_start(
                    out=w_planes[32 * quadrant : 32 * quadrant + 4, l, :].bitcast(I32),
                    in_=scales.rearrange("g q o -> (g q) o")[4 * quadrant : 4 * quadrant + 4, :].bitcast(I32),
                )

        def transpose_half(s):
            x_words = x_tiles[s // 2][:].bitcast(F32).rearrange("n (p t j) -> n t j p", t=PACK, j=PAIRS)
            xt_banks[s] = []
            for b in range(HALF // 2):
                j = first_channel(s) // 2 + b
                xt = xt_psum.tile([P, PACK, P], F32)
                for t in range(PACK):
                    nc.tensor.transpose(xt[:, t, :], x_words[:, t, j, :], identity[:])
                xt_banks[s].append(xt)

        def split_half(s):
            grouped = mx_pool.tile([P, HALF, P, PACK], BF16, align_bytes=64)
            grouped_tiles[s] = grouped
            for b, xt in enumerate(xt_banks[s]):
                split = xt[:].bitcast(BF16).rearrange("p t (n e) -> p e n t", e=2)
                if b % 2 == 0:
                    nc.vector.tensor_copy(out=grouped[:, 2 * b : 2 * b + 2, :, :], in_=split)
                else:
                    nc.scalar.copy(out=grouped[:, 2 * b : 2 * b + 2, :, :], in_=split)

        def quantise_half(s, calls=1):
            codes = mx_pool.tile([P, HALF, P], U32, align_bytes=64)
            planes = mx_pool.tile([P, HALF, P], U8, align_bytes=64)
            code_tiles[s] = (codes, planes)
            for part in range(calls):
                channels = slice(part * HALF // calls, (part + 1) * HALF // calls)
                nc.vector.quantize_mx(
                    out=codes[:, channels, :].rearrange("p c n -> p (c n)").bitcast(FP8X4),
                    scales=planes[:, channels, :].rearrange("p c n -> p (c n)"),
                    in_=grouped_tiles[s][:, channels, :, :].rearrange("p c n t -> p (c n t)"),
                )

        def multiply_half(s):
            codes, planes = code_tiles[s]
            acc_banks[s] = []
            for q in range(HALF // QUAD):
                if s >= STEPS - 2:
                    acc = xt_psum.tile([P, QUAD, OUTS], F32, name="xt")
                else:
                    acc = acc_psum.tile([P, QUAD, OUTS], F32)
                for m in range(QUAD):
                    c = QUAD * q + m
                    l = DEGREE_OF_CHANNEL[first_channel(s) + c]
                    nc.tensor.matmul_mx(
                        out=acc[:, m, :],
                        lhsT=codes[:, c, :].bitcast(FP8X4),
                        lhsT_scale=planes[:, c, :],
                        rhs=w_codes[:, l, :].bitcast(FP8X4),
                        rhs_scale=w_planes[:, l, :],
                        start=True,
                        stop=True,
                    )
                acc_banks[s].append(acc)

        def store_half(s):
            r = s // 2
            if s % 2 == 0:
                out_sb = out_pool.tile([P, OUTS, CHANNELS], F32)
                out_tiles[r] = out_sb
            for q, acc in enumerate(acc_banks[s]):
                first = first_channel(s) + QUAD * q
                nc.scalar.copy(out=out_tiles[r][:, :, first : first + QUAD], in_=acc[:].rearrange("p c o -> p o c"))
            if s % 2 == 1:
                nc.sync.dma_start(
                    out=out[r * P : (r + 1) * P].rearrange("n o c -> n (o c)"),
                    in_=out_tiles[r][:].rearrange("p o c -> p (o c)"),
                )

        def store_last():
            s, r = STEPS - 1, ROW_TILES - 1
            first = first_channel(s)
            nc.scalar.copy(
                out=out_tiles[r][:, :, first : first + QUAD], in_=acc_banks[s][0][:].rearrange("p c o -> p o c")
            )
            first += QUAD
            for h in range(2):
                o = slice(h * OUTS // 2, (h + 1) * OUTS // 2)
                nc.vector.tensor_copy(
                    out=out_tiles[r][:, o, first : first + QUAD],
                    in_=acc_banks[s][1][:, :, o].rearrange("p c o -> p o c"),
                )
                nc.sync.dma_start(
                    out=out[r * P : (r + 1) * P, o, :].rearrange("n o c -> n (o c)"),
                    in_=out_tiles[r][:, o, :].rearrange("p o c -> p (o c)"),
                )

        identity = keep.tile([P, P], F32)
        make_identity(nc, identity[:])
        load_rows(0)
        load_weight(2)
        load_rows(1)
        load_weight(3)
        load_rows(2)
        load_weight(0)
        load_weight(1)
        for r in range(3, ROW_TILES):
            load_rows(r)
        ctx.enter_context(tc.manual_schedule())
        transpose_half(0)

        for s in range(STEPS):
            if s >= 2:
                multiply_half(s - 2)
            if s + 1 < STEPS:
                transpose_half(s + 1)
            split_half(s)
            if s >= 1:
                quantise_half(s - 1)
            if s >= 2:
                store_half(s - 2)
        multiply_half(STEPS - 2)
        quantise_half(STEPS - 1, calls=2)
        store_half(STEPS - 2)
        multiply_half(STEPS - 1)
        store_last()
